import numpy as np
import ml_dtypes


def mxq(x, axis, fmt="e4m3"):
    dtype, down = {"e4m3": (ml_dtypes.float8_e4m3fn, 7), "e5m2": (ml_dtypes.float8_e5m2, 14)}[fmt]
    v = np.moveaxis(np.asarray(x, np.float32).astype(ml_dtypes.bfloat16).astype(np.float64), axis, -1)
    blocks = v.reshape(v.shape[:-1] + (-1, 32))
    amax = np.abs(blocks).max(-1, keepdims=True)
    byte = np.maximum(np.where(amax > 0, np.frexp(amax)[1] - 1 + 127, 0) - down, 1)
    scale = np.exp2(byte - 127.0)
    codes = (blocks / scale).astype(np.float32).astype(dtype).astype(np.float64)
    return np.moveaxis((codes * scale).reshape(v.shape), -1, axis)


WIDE = False


def mx_kscale(k):
    if not WIDE:
        return np.ones(k)
    levels = np.array([10, -10, 5, -5, 0])
    a = np.random.permutation(np.resize(levels, k // 512 * 4)).reshape(k // 512, 4)
    idx = np.arange(k)
    return np.exp2(a[idx // 512, idx % 128 // 32])


BF16 = ml_dtypes.bfloat16


def bf(x):
    return np.asarray(x, np.float32).astype(BF16)


def f64(x):
    return np.asarray(x).astype(np.float64)


B, D_IN, D_H = 512, 1024, 1024


def sigmoid(v):
    return 1.0 / (1.0 + np.exp(-v))


def setup_inputs():
    s, t = mx_kscale(D_IN), mx_kscale(D_H)

    def w_in():
        return bf(np.random.standard_normal((D_H, D_IN)) * 0.6 / np.sqrt(D_IN) / s[None, :])

    def w_rec():
        return bf(np.random.standard_normal((D_H, D_H)) * 0.6 / np.sqrt(D_H) / t[None, :])

    def bias():
        return bf(np.random.standard_normal(D_H) * 0.3)

    return {"incoming": bf(np.random.standard_normal((B, D_IN)) * s), "h": bf(np.random.standard_normal((B, D_H)) * t),
            "c": bf(np.random.standard_normal((B, D_H))), "gated_cand": bf(np.random.standard_normal((B, D_H)) * 0.5),
            "W_f": w_in(), "b_W_f": bias(), "W_o": w_in(), "b_W_o": bias(),
            "U_f": w_rec(), "b_U_f": bias(), "U_o": w_rec(), "b_U_o": bias()}


def reference(incoming, h, c, gated_cand, W_f, b_W_f, W_o, b_W_o, U_f, b_U_f, U_o, b_U_o):
    xq = mxq(f64(incoming), 1, "e4m3")
    hq = mxq(f64(h), 1, "e4m3")
    O = sigmoid((xq @ mxq(f64(W_o), 1, "e4m3").T) + f64(b_W_o) + (hq @ mxq(f64(U_o), 1, "e4m3").T) + f64(b_U_o))
    F = sigmoid((xq @ mxq(f64(W_f), 1, "e4m3").T) + f64(b_W_f) + (hq @ mxq(f64(U_f), 1, "e4m3").T) + f64(b_U_f))
    C = F * f64(c) + f64(gated_cand)
    H = O * np.tanh(C)
    return (H, C)

@@ -1,0 +1,218 @@
+from contextlib import ExitStack
+
+import concourse.mybir as mybir
+from concourse.masks import make_identity
+
+F32 = mybir.dt.float32
+BF16 = mybir.dt.bfloat16
+U32 = mybir.dt.uint32
+U8 = mybir.dt.uint8
+FP8X4 = mybir.dt.float8_e4m3fn_x4
+ACT = mybir.ActivationFunctionType
+ALU = mybir.AluOpType
+
+P = 128
+BATCH = 512
+FEATURES = 1024
+PACK = 4
+K_PASS = P * PACK
+PASSES = FEATURES // K_PASS
+PAIRS = 2
+ROWS = 512
+ROW_BLOCKS = ROWS // P
+BATCH_TILES = BATCH // P
+HALVES = FEATURES // ROWS
+GATES = 2
+LAST_GROUP = GATES * HALVES - 1
+SHARED_COPIES = 2
+
+MULTIPLY_LAG = 1
+SIGMOID_LAG = 2
+HIDDEN_LAG = 3
+SUM_LAG = 4
+TANH_LAG = 5
+
+FLOPS = 2 * BATCH * (2 * FEATURES) * (GATES * FEATURES)
+
+PIN = True
+
+
+def tile_lstmcell_pb_kernel(
+    tc, incoming, h, c, gated_cand, W_f, b_W_f, W_o, b_W_o, U_f, b_U_f, U_o, b_U_o, out_0, out_1
+):
+    nc = tc.nc
+    with ExitStack() as ctx:
+        const = ctx.enter_context(tc.tile_pool(name="const", bufs=1))
+        raw_pool = ctx.enter_context(tc.tile_pool(name="raw", bufs=1))
+        grouped_pool = ctx.enter_context(tc.tile_pool(name="grouped", bufs=3))
+        act_pool = ctx.enter_context(tc.tile_pool(name="act", bufs=2))
+        weight_pool = ctx.enter_context(tc.tile_pool(name="weight", bufs=3))
+        gate_pool = ctx.enter_context(tc.tile_pool(name="gate", bufs=12))
+        cell_pool = ctx.enter_context(tc.tile_pool(name="cell", bufs=8))
+        tanh_pool = ctx.enter_context(tc.tile_pool(name="tanh", bufs=8))
+        transposed = ctx.enter_context(tc.psum_pool(name="transposed", bufs=4))
+        sums = ctx.enter_context(tc.psum_pool(name="sums", bufs=1))
+        if PIN:
+            ctx.enter_context(tc.manual_schedule())
+
+        ident = const.tile([P, P], F32, name="ident")
+        make_identity(nc, ident[:])
+        ones = const.tile([P, P], BF16, name="ones")
+        nc.vector.memset(ones[:], 1.0)
+        warm = const.tile([P, 1], F32, name="warm")
+        nc.vector.memset(warm[:], 0.0)
+        nc.scalar.activation(out=warm[:], in_=warm[:], func=ACT.Sigmoid)
+        bias_rows = const.tile([P, GATES * FEATURES], BF16, name="bias_rows")
+        nc.vector.memset(bias_rows[:], 0.0)
+        for gate, pair in enumerate(((b_W_f, b_U_f), (b_W_o, b_U_o))):
+            for row, vector in enumerate(pair):
+                nc.scalar.dma_start(
+                    out=bias_rows[row : row + 1, gate * FEATURES : (gate + 1) * FEATURES],
+                    in_=vector.rearrange("(o n) -> o n", o=1),
+                )
+
+        gate_weights = ((W_f, U_f), (W_o, U_o))
+        weight_chunks = []
+        for group in range(GATES * HALVES):
+            gate, half = divmod(group, HALVES)
+            for source in range(2):
+                rows = gate_weights[gate][source][half * ROWS : (half + 1) * ROWS, :]
+                weight_chunks.append({"name": "w%d%d" % (group, source), "rows": rows, "source": source, "group": group})
+        x_chunk = {"name": "x", "rows": incoming, "source": 0, "group": None}
+        h_chunk = {"name": "h", "rows": h, "source": 1, "group": None}
+        acts = (x_chunk, h_chunk)
+        chunks = [x_chunk, weight_chunks[0], h_chunk] + weight_chunks[1:]
+
+        c_sb = raw_pool.tile([P, BATCH_TILES, FEATURES], BF16, name="c_sb")
+        g_sb = raw_pool.tile([P, BATCH_TILES, FEATURES], BF16, name="g_sb")
+        first_output_chunk = weight_chunks[2 * HALVES]
+        for chunk in chunks:
+            if chunk is first_output_chunk:
+                nc.sync.dma_start(out=c_sb[:], in_=c.rearrange("(b p) n -> p b n", p=P))
+            chunk["raw"] = []
+            for rb in range(ROW_BLOCKS):
+                raw = raw_pool.tile([P, FEATURES], BF16, name="raw_%s_%d" % (chunk["name"], rb))
+                nc.sync.dma_start(out=raw[:], in_=chunk["rows"][rb * P : (rb + 1) * P, :])
+                chunk["raw"].append(raw)
+            if chunk is first_output_chunk:
+                nc.sync.dma_start(out=g_sb[:], in_=gated_cand.rearrange("(b p) n -> p b n", p=P))
+
+        def new_sums():
+            return [sums.tile([P, ROWS], F32, name="sum%d" % b) for b in range(BATCH_TILES)]
+
+        def transpose_chunk(chunk, vector_copies):
+            grouped = grouped_pool.tile([P, PASSES * ROWS * PACK], BF16, name="grouped", align_bytes=64)
+            grouped_words = grouped[:].bitcast(F32).rearrange("p (g r u) -> p g r u", g=PASSES, u=PAIRS)
+            for rb in range(ROW_BLOCKS):
+                raw_words = chunk["raw"][rb][:].bitcast(F32)
+                bank = transposed.tile([P, PASSES, PAIRS, P], F32, name="bank")
+                for g in range(PASSES):
+                    for u in range(PAIRS):
+                        first = (g * PAIRS + u) * P
+                        nc.tensor.transpose(bank[:, g, u, :], raw_words[:, first : first + P], ident[:])
+                copy_out = nc.vector.tensor_copy if rb >= ROW_BLOCKS - vector_copies else nc.scalar.copy
+                copy_out(
+                    out=grouped_words[:, :, rb * P : (rb + 1) * P, :],
+                    in_=bank[:].rearrange("p g u r -> p g r u"),
+                )
+            chunk["grouped"] = grouped
+
+        def quantise_chunk(chunk):
+            pool = act_pool if chunk["group"] is None else weight_pool
+            codes = pool.tile([P, PASSES * ROWS], U32, name="codes", align_bytes=64)
+            scales = pool.tile([P, PASSES * ROWS], U8, name="scales", align_bytes=64)
+            nc.vector.quantize_mx(out=codes[:].bitcast(FP8X4), scales=scales[:], in_=chunk["grouped"][:])
+            chunk["codes"] = codes
+            chunk["scales"] = scales
+
+        def multiply_chunk(chunk, acc):
+            act = acts[chunk["source"]]
+            for b in range(BATCH_TILES):
+                for g in range(PASSES):
+                    m_cols = slice(g * ROWS + b * P, g * ROWS + (b + 1) * P)
+                    n_cols = slice(g * ROWS, (g + 1) * ROWS)
+                    nc.tensor.matmul_mx(
+                        out=acc[b][:],
+                        lhsT=act["codes"][:, m_cols].bitcast(FP8X4),
+                        lhsT_scale=act["scales"][:, m_cols],
+                        rhs=chunk["codes"][:, n_cols].bitcast(FP8X4),
+                        rhs_scale=chunk["scales"][:, n_cols],
+                        start=(chunk["source"] == 0 and g == 0),
+                        stop=(chunk["source"] == 1 and g == PASSES - 1),
+                    )
+
+        def closing(index):
+            if 0 <= index < len(chunks) and chunks[index]["group"] is not None and chunks[index]["source"] == 1:
+                return chunks[index]["group"]
+            return None
+
+        bias_sb = const.tile([P, GATES * FEATURES], F32, name="bias_sb")
+        acc = {}
+        gates = {}
+        cells = {}
+        tanhs = {}
+
+        for step in range(len(chunks) + SIGMOID_LAG):
+            if step < len(chunks):
+                transpose_chunk(chunks[step], SHARED_COPIES if closing(step - MULTIPLY_LAG) is None else 0)
+            if step == 0:
+                for q, bank in enumerate(new_sums()):
+                    nc.tensor.matmul(out=bank[:], lhsT=ones[:], rhs=bias_rows[:, q * ROWS : (q + 1) * ROWS], start=True, stop=True)
+                    nc.scalar.copy(out=bias_sb[:, q * ROWS : (q + 1) * ROWS], in_=bank[:])
+
+            group = closing(step - SIGMOID_LAG)
+            if group is not None:
+                gate, half = divmod(group, HALVES)
+                cols = slice(half * ROWS, (half + 1) * ROWS)
+                for b in range(BATCH_TILES):
+                    nc.scalar.activation(out=gates[group][b][:], in_=gates[group][b][:], func=ACT.Sigmoid)
+                if gate == 0:
+                    cells[half] = [cell_pool.tile([P, ROWS], F32, name="cell") for b in range(BATCH_TILES)]
+                    for b in range(BATCH_TILES):
+                        nc.gpsimd.tensor_tensor(out=gates[group][b][:], in0=gates[group][b][:], in1=c_sb[:, b, cols], op=ALU.mult)
+                    for b in range(0, BATCH_TILES, 2):
+                        nc.gpsimd.tensor_tensor(out=cells[half][b][:], in0=gates[group][b][:], in1=g_sb[:, b, cols], op=ALU.add)
+
+            group = closing(step - TANH_LAG)
+            if group is not None and group < HALVES:
+                half = group
+                cols = slice(half * ROWS, (half + 1) * ROWS)
+                tanhs[half] = [tanh_pool.tile([P, ROWS], F32, name="tanh_c") for b in range(BATCH_TILES)]
+                for b in range(BATCH_TILES):
+                    nc.scalar.activation(out=tanhs[half][b][:], in_=cells[half][b][:], func=ACT.Tanh)
+                    nc.sync.dma_start(out=out_1[b * P : (b + 1) * P, cols], in_=cells[half][b][:])
+
+            before = step - MULTIPLY_LAG
+            if 0 <= before < len(chunks) and chunks[before]["group"] is not None:
+                group = chunks[before]["group"]
+                if chunks[before]["source"] == 0:
+                    acc[group] = new_sums()
+                multiply_chunk(chunks[before], acc[group])
+
+            if step < len(chunks):
+                quantise_chunk(chunks[step])
+
+            group = closing(step - MULTIPLY_LAG)
+            if group is not None:
+                gates[group] = [gate_pool.tile([P, ROWS], F32, name="gate") for b in range(BATCH_TILES)]
+                for b in range(BATCH_TILES):
+                    nc.vector.tensor_tensor(
+                        out=gates[group][b][:], in0=acc[group][b][:],
+                        in1=bias_sb[:, group * ROWS : (group + 1) * ROWS], op=ALU.add,
+                    )
+
+            group = closing(step - SUM_LAG)
+            if group is not None and group < HALVES:
+                half = group
+                cols = slice(half * ROWS, (half + 1) * ROWS)
+                for b in range(1, BATCH_TILES, 2):
+                    nc.vector.tensor_tensor(out=cells[half][b][:], in0=gates[group][b][:], in1=g_sb[:, b, cols], op=ALU.add)
+
+            for engine, group in ((nc.gpsimd, closing(step - HIDDEN_LAG)), (nc.vector, closing(step - SIGMOID_LAG))):
+                if group is None or group < HALVES or (group == LAST_GROUP) != (engine is nc.vector):
+                    continue
+                half = group - HALVES
+                cols = slice(half * ROWS, (half + 1) * ROWS)
+                for b in range(BATCH_TILES):
+                    engine.tensor_tensor(out=gates[group][b][:], in0=gates[group][b][:], in1=tanhs[half][b][:], op=ALU.mult)
+                    nc.sync.dma_start(out=out_0[b * P : (b + 1) * P, cols], in_=gates[group][b][:])

@@ -28,8 +28,8 @@ SHARED_COPIES = 2
 
 MULTIPLY_LAG = 1
 SIGMOID_LAG = 2
-HIDDEN_LAG = 3
-SUM_LAG = 4
+FIRST_CLOSING = 3
+SUM_LAG = 3
 TANH_LAG = 5
 
 FLOPS = 2 * BATCH * (2 * FEATURES) * (GATES * FEATURES)
@@ -154,7 +154,7 @@ def tile_lstmcell_pb_kernel(
 
         for step in range(len(chunks) + SIGMOID_LAG):
             if step < len(chunks):
-                transpose_chunk(chunks[step], SHARED_COPIES if closing(step - MULTIPLY_LAG) is None else 0)
+                transpose_chunk(chunks[step], SHARED_COPIES if step <= FIRST_CLOSING else 0)
             if step == 0:
                 for q, bank in enumerate(new_sums()):
                     nc.tensor.matmul(out=bank[:], lhsT=ones[:], rhs=bias_rows[:, q * ROWS : (q + 1) * ROWS], start=True, stop=True)
@@ -162,16 +162,8 @@ def tile_lstmcell_pb_kernel(
 
             group = closing(step - SIGMOID_LAG)
             if group is not None:
-                gate, half = divmod(group, HALVES)
-                cols = slice(half * ROWS, (half + 1) * ROWS)
                 for b in range(BATCH_TILES):
                     nc.scalar.activation(out=gates[group][b][:], in_=gates[group][b][:], func=ACT.Sigmoid)
-                if gate == 0:
-                    cells[half] = [cell_pool.tile([P, ROWS], F32, name="cell") for b in range(BATCH_TILES)]
-                    for b in range(BATCH_TILES):
-                        nc.gpsimd.tensor_tensor(out=gates[group][b][:], in0=gates[group][b][:], in1=c_sb[:, b, cols], op=ALU.mult)
-                    for b in range(0, BATCH_TILES, 2):
-                        nc.gpsimd.tensor_tensor(out=cells[half][b][:], in0=gates[group][b][:], in1=g_sb[:, b, cols], op=ALU.add)
 
             group = closing(step - TANH_LAG)
             if group is not None and group < HALVES:
@@ -205,14 +197,21 @@ def tile_lstmcell_pb_kernel(
             if group is not None and group < HALVES:
                 half = group
                 cols = slice(half * ROWS, (half + 1) * ROWS)
-                for b in range(1, BATCH_TILES, 2):
+                cells[half] = [cell_pool.tile([P, ROWS], F32, name="cell") for b in range(BATCH_TILES)]
+                for b in range(BATCH_TILES):
                     nc.vector.tensor_tensor(out=cells[half][b][:], in0=gates[group][b][:], in1=g_sb[:, b, cols], op=ALU.add)
 
-            for engine, group in ((nc.gpsimd, closing(step - HIDDEN_LAG)), (nc.vector, closing(step - SIGMOID_LAG))):
-                if group is None or group < HALVES or (group == LAST_GROUP) != (engine is nc.vector):
-                    continue
+            group = closing(step - SIGMOID_LAG)
+            if group is not None and group < HALVES:
+                half = group
+                cols = slice(half * ROWS, (half + 1) * ROWS)
+                for b in range(BATCH_TILES):
+                    nc.vector.tensor_tensor(out=gates[group][b][:], in0=gates[group][b][:], in1=c_sb[:, b, cols], op=ALU.mult)
+
+            group = closing(step - SIGMOID_LAG)
+            if group is not None and group >= HALVES:
                 half = group - HALVES
                 cols = slice(half * ROWS, (half + 1) * ROWS)
                 for b in range(BATCH_TILES):
-                    engine.tensor_tensor(out=gates[group][b][:], in0=gates[group][b][:], in1=tanhs[half][b][:], op=ALU.mult)
+                    nc.vector.tensor_tensor(out=gates[group][b][:], in0=gates[group][b][:], in1=tanhs[half][b][:], op=ALU.mult)
                     nc.sync.dma_start(out=out_0[b * P : (b + 1) * P, cols], in_=gates[group][b][:])

@@ -18,23 +18,25 @@ PACK = 4
 K_PASS = P * PACK
 PASSES = FEATURES // K_PASS
 PAIRS = 2
-ROWS = 512
-ROW_BLOCKS = ROWS // P
-BATCH_TILES = BATCH // P
-HALVES = FEATURES // ROWS
+SOURCES = 2
 GATES = 2
-LAST_GROUP = GATES * HALVES - 1
+BATCH_TILES = BATCH // P
+WIDTH = 256
+ROUNDS_PER_GATE = FEATURES // WIDTH
+ROUNDS = GATES * ROUNDS_PER_GATE
+BLOCKS = 4
+BANK = 512
+TILES_PER_BANK = BANK // WIDTH
+BANKS = BATCH_TILES // TILES_PER_BANK
+HEAD_UNITS = 3
 SHARED_COPIES = 2
 
 MULTIPLY_LAG = 1
 SIGMOID_LAG = 2
-FIRST_CLOSING = 3
 SUM_LAG = 3
-TANH_LAG = 5
+TANH_LAG = 4
 
-FLOPS = 2 * BATCH * (2 * FEATURES) * (GATES * FEATURES)
-
-PIN = True
+FLOPS = 2 * BATCH * (SOURCES * FEATURES) * (GATES * FEATURES)
 
 
 def tile_lstmcell_pb_kernel(
@@ -45,15 +47,14 @@ def tile_lstmcell_pb_kernel(
         const = ctx.enter_context(tc.tile_pool(name="const", bufs=1))
         raw_pool = ctx.enter_context(tc.tile_pool(name="raw", bufs=1))
         grouped_pool = ctx.enter_context(tc.tile_pool(name="grouped", bufs=3))
-        act_pool = ctx.enter_context(tc.tile_pool(name="act", bufs=2))
+        act_pool = ctx.enter_context(tc.tile_pool(name="act", bufs=SOURCES))
         weight_pool = ctx.enter_context(tc.tile_pool(name="weight", bufs=3))
-        gate_pool = ctx.enter_context(tc.tile_pool(name="gate", bufs=12))
+        gate_pool = ctx.enter_context(tc.tile_pool(name="gate", bufs=10))
         cell_pool = ctx.enter_context(tc.tile_pool(name="cell", bufs=8))
         tanh_pool = ctx.enter_context(tc.tile_pool(name="tanh", bufs=8))
         transposed = ctx.enter_context(tc.psum_pool(name="transposed", bufs=4))
-        sums = ctx.enter_context(tc.psum_pool(name="sums", bufs=1))
-        if PIN:
-            ctx.enter_context(tc.manual_schedule())
+        sums = ctx.enter_context(tc.psum_pool(name="sums", bufs=4))
+        ctx.enter_context(tc.manual_schedule())
 
         ident = const.tile([P, P], F32, name="ident")
         make_identity(nc, ident[:])
@@ -72,146 +73,141 @@ def tile_lstmcell_pb_kernel(
                 )
 
         gate_weights = ((W_f, U_f), (W_o, U_o))
-        weight_chunks = []
-        for group in range(GATES * HALVES):
-            gate, half = divmod(group, HALVES)
-            for source in range(2):
-                rows = gate_weights[gate][source][half * ROWS : (half + 1) * ROWS, :]
-                weight_chunks.append({"name": "w%d%d" % (group, source), "rows": rows, "source": source, "group": group})
-        x_chunk = {"name": "x", "rows": incoming, "source": 0, "group": None}
-        h_chunk = {"name": "h", "rows": h, "source": 1, "group": None}
-        acts = (x_chunk, h_chunk)
-        chunks = [x_chunk, weight_chunks[0], h_chunk] + weight_chunks[1:]
+        units = []
+        for name, matrix in (("x", incoming), ("h", h)):
+            blocks = [{"rows": matrix[i * P : (i + 1) * P, :], "slot": 0, "column": i * P} for i in range(BLOCKS)]
+            units.append({"name": name, "blocks": blocks, "slots": PASSES, "width": BATCH})
+        for number in range(ROUNDS):
+            gate, part = divmod(number, ROUNDS_PER_GATE)
+            blocks = []
+            for source in range(SOURCES):
+                for i in range(WIDTH // P):
+                    first = part * WIDTH + i * P
+                    blocks.append({"rows": gate_weights[gate][source][first : first + P, :], "slot": source * PASSES, "column": i * P})
+            units.append({"name": "r%d" % number, "blocks": blocks, "slots": SOURCES * PASSES, "width": WIDTH})
+        first_round = len(units) - ROUNDS
 
         c_sb = raw_pool.tile([P, BATCH_TILES, FEATURES], BF16, name="c_sb")
         g_sb = raw_pool.tile([P, BATCH_TILES, FEATURES], BF16, name="g_sb")
-        first_output_chunk = weight_chunks[2 * HALVES]
-        for chunk in chunks:
-            if chunk is first_output_chunk:
+        for index, unit in enumerate(units):
+            for i, block in enumerate(unit["blocks"]):
+                raw = raw_pool.tile([P, FEATURES], BF16, name="raw_%s_%d" % (unit["name"], i))
+                nc.sync.dma_start(out=raw[:], in_=block["rows"])
+                block["raw"] = raw
+            if index == first_round + 1:
                 nc.sync.dma_start(out=c_sb[:], in_=c.rearrange("(b p) n -> p b n", p=P))
-            chunk["raw"] = []
-            for rb in range(ROW_BLOCKS):
-                raw = raw_pool.tile([P, FEATURES], BF16, name="raw_%s_%d" % (chunk["name"], rb))
-                nc.sync.dma_start(out=raw[:], in_=chunk["rows"][rb * P : (rb + 1) * P, :])
-                chunk["raw"].append(raw)
-            if chunk is first_output_chunk:
+            if index == first_round + 2:
                 nc.sync.dma_start(out=g_sb[:], in_=gated_cand.rearrange("(b p) n -> p b n", p=P))
 
-        def new_sums():
-            return [sums.tile([P, ROWS], F32, name="sum%d" % b) for b in range(BATCH_TILES)]
-
-        def transpose_chunk(chunk, vector_copies):
-            grouped = grouped_pool.tile([P, PASSES * ROWS * PACK], BF16, name="grouped", align_bytes=64)
-            grouped_words = grouped[:].bitcast(F32).rearrange("p (g r u) -> p g r u", g=PASSES, u=PAIRS)
-            for rb in range(ROW_BLOCKS):
-                raw_words = chunk["raw"][rb][:].bitcast(F32)
+        def transpose_unit(unit, vector_copies):
+            grouped = grouped_pool.tile([P, BLOCKS * FEATURES], BF16, name="grouped", align_bytes=64)
+            grouped_words = grouped[:].bitcast(F32).rearrange("p (s r u) -> p s r u", s=unit["slots"], u=PAIRS)
+            for i, block in enumerate(unit["blocks"]):
+                raw_words = block["raw"][:].bitcast(F32)
                 bank = transposed.tile([P, PASSES, PAIRS, P], F32, name="bank")
                 for g in range(PASSES):
                     for u in range(PAIRS):
                         first = (g * PAIRS + u) * P
                         nc.tensor.transpose(bank[:, g, u, :], raw_words[:, first : first + P], ident[:])
-                copy_out = nc.vector.tensor_copy if rb >= ROW_BLOCKS - vector_copies else nc.scalar.copy
+                copy_out = nc.vector.tensor_copy if i >= BLOCKS - vector_copies else nc.scalar.copy
                 copy_out(
-                    out=grouped_words[:, :, rb * P : (rb + 1) * P, :],
+                    out=grouped_words[:, block["slot"] : block["slot"] + PASSES, block["column"] : block["column"] + P, :],
                     in_=bank[:].rearrange("p g u r -> p g r u"),
                 )
-            chunk["grouped"] = grouped
+            unit["grouped"] = grouped
 
-        def quantise_chunk(chunk):
-            pool = act_pool if chunk["group"] is None else weight_pool
-            codes = pool.tile([P, PASSES * ROWS], U32, name="codes", align_bytes=64)
-            scales = pool.tile([P, PASSES * ROWS], U8, name="scales", align_bytes=64)
-            nc.vector.quantize_mx(out=codes[:].bitcast(FP8X4), scales=scales[:], in_=chunk["grouped"][:])
-            chunk["codes"] = codes
-            chunk["scales"] = scales
+        def quantise_unit(unit, pool):
+            codes = pool.tile([P, BLOCKS * FEATURES // PACK], U32, name="codes", align_bytes=64)
+            scales = pool.tile([P, BLOCKS * FEATURES // PACK], U8, name="scales", align_bytes=64)
+            nc.vector.quantize_mx(out=codes[:].bitcast(FP8X4), scales=scales[:], in_=unit["grouped"][:])
+            unit["codes"] = codes
+            unit["scales"] = scales
 
-        def multiply_chunk(chunk, acc):
-            act = acts[chunk["source"]]
-            for b in range(BATCH_TILES):
-                for g in range(PASSES):
-                    m_cols = slice(g * ROWS + b * P, g * ROWS + (b + 1) * P)
-                    n_cols = slice(g * ROWS, (g + 1) * ROWS)
-                    nc.tensor.matmul_mx(
-                        out=acc[b][:],
-                        lhsT=act["codes"][:, m_cols].bitcast(FP8X4),
-                        lhsT_scale=act["scales"][:, m_cols],
-                        rhs=chunk["codes"][:, n_cols].bitcast(FP8X4),
-                        rhs_scale=chunk["scales"][:, n_cols],
-                        start=(chunk["source"] == 0 and g == 0),
-                        stop=(chunk["source"] == 1 and g == PASSES - 1),
-                    )
+        def multiply_round(unit):
+            unit["sums"] = []
+            for t in range(BANKS):
+                bank = sums.tile([P, TILES_PER_BANK, WIDTH], F32, name="sum")
+                for j in range(TILES_PER_BANK):
+                    b = t * TILES_PER_BANK + j
+                    for slot in range(SOURCES * PASSES):
+                        source, g = divmod(slot, PASSES)
+                        m_cols = slice(g * BATCH + b * P, g * BATCH + (b + 1) * P)
+                        n_cols = slice(slot * WIDTH, (slot + 1) * WIDTH)
+                        nc.tensor.matmul_mx(
+                            out=bank[:, j, :],
+                            lhsT=units[source]["codes"][:, m_cols].bitcast(FP8X4),
+                            lhsT_scale=units[source]["scales"][:, m_cols],
+                            rhs=unit["codes"][:, n_cols].bitcast(FP8X4),
+                            rhs_scale=unit["scales"][:, n_cols],
+                            start=(slot == 0),
+                            stop=(slot == SOURCES * PASSES - 1),
+                        )
+                unit["sums"].append(bank)
 
-        def closing(index):
-            if 0 <= index < len(chunks) and chunks[index]["group"] is not None and chunks[index]["source"] == 1:
-                return chunks[index]["group"]
-            return None
+        def round_at(step, lag):
+            number = step - lag - first_round
+            return number if 0 <= number < ROUNDS else None
+
+        def rows_of(t):
+            return slice(t * TILES_PER_BANK, (t + 1) * TILES_PER_BANK)
 
         bias_sb = const.tile([P, GATES * FEATURES], F32, name="bias_sb")
-        acc = {}
+        out_h = out_0.rearrange("(b p) n -> p b n", p=P)
+        out_c = out_1.rearrange("(b p) n -> p b n", p=P)
         gates = {}
         cells = {}
         tanhs = {}
 
-        for step in range(len(chunks) + SIGMOID_LAG):
-            if step < len(chunks):
-                transpose_chunk(chunks[step], SHARED_COPIES if step <= FIRST_CLOSING else 0)
+        for step in range(len(units) + SIGMOID_LAG):
+            if step < len(units):
+                transpose_unit(units[step], SHARED_COPIES if step < HEAD_UNITS else 0)
             if step == 0:
-                for q, bank in enumerate(new_sums()):
-                    nc.tensor.matmul(out=bank[:], lhsT=ones[:], rhs=bias_rows[:, q * ROWS : (q + 1) * ROWS], start=True, stop=True)
-                    nc.scalar.copy(out=bias_sb[:, q * ROWS : (q + 1) * ROWS], in_=bank[:])
+                for q in range(GATES * FEATURES // BANK):
+                    bank = sums.tile([P, BANK], F32, name="sum")
+                    nc.tensor.matmul(out=bank[:], lhsT=ones[:], rhs=bias_rows[:, q * BANK : (q + 1) * BANK], start=True, stop=True)
+                    nc.scalar.copy(out=bias_sb[:, q * BANK : (q + 1) * BANK], in_=bank[:])
 
-            group = closing(step - SIGMOID_LAG)
-            if group is not None:
-                for b in range(BATCH_TILES):
-                    nc.scalar.activation(out=gates[group][b][:], in_=gates[group][b][:], func=ACT.Sigmoid)
+            number = round_at(step, SIGMOID_LAG)
+            if number is not None:
+                for t in range(BANKS):
+                    nc.scalar.activation(out=gates[number][t][:], in_=gates[number][t][:], func=ACT.Sigmoid)
 
-            group = closing(step - TANH_LAG)
-            if group is not None and group < HALVES:
-                half = group
-                cols = slice(half * ROWS, (half + 1) * ROWS)
-                tanhs[half] = [tanh_pool.tile([P, ROWS], F32, name="tanh_c") for b in range(BATCH_TILES)]
-                for b in range(BATCH_TILES):
-                    nc.scalar.activation(out=tanhs[half][b][:], in_=cells[half][b][:], func=ACT.Tanh)
-                    nc.sync.dma_start(out=out_1[b * P : (b + 1) * P, cols], in_=cells[half][b][:])
+            number = round_at(step, TANH_LAG)
+            if number is not None and number < ROUNDS_PER_GATE:
+                cols = slice(number * WIDTH, (number + 1) * WIDTH)
+                tanhs[number] = [tanh_pool.tile([P, TILES_PER_BANK, WIDTH], F32, name="tanh_c") for t in range(BANKS)]
+                for t in range(BANKS):
+                    nc.scalar.activation(out=tanhs[number][t][:], in_=cells[number][t][:], func=ACT.Tanh)
+                    nc.sync.dma_start(out=out_c[:, rows_of(t), cols], in_=cells[number][t][:])
 
-            before = step - MULTIPLY_LAG
-            if 0 <= before < len(chunks) and chunks[before]["group"] is not None:
-                group = chunks[before]["group"]
-                if chunks[before]["source"] == 0:
-                    acc[group] = new_sums()
-                multiply_chunk(chunks[before], acc[group])
+            number = round_at(step, MULTIPLY_LAG)
+            if number is not None:
+                multiply_round(units[first_round + number])
 
-            if step < len(chunks):
-                quantise_chunk(chunks[step])
+            if step < len(units):
+                quantise_unit(units[step], act_pool if step < first_round else weight_pool)
 
-            group = closing(step - MULTIPLY_LAG)
-            if group is not None:
-                gates[group] = [gate_pool.tile([P, ROWS], F32, name="gate") for b in range(BATCH_TILES)]
-                for b in range(BATCH_TILES):
-                    nc.vector.tensor_tensor(
-                        out=gates[group][b][:], in0=acc[group][b][:],
-                        in1=bias_sb[:, group * ROWS : (group + 1) * ROWS], op=ALU.add,
-                    )
+            if number is not None:
+                bias_cols = bias_sb[:, number * WIDTH : (number + 1) * WIDTH].unsqueeze(1).to_broadcast([P, TILES_PER_BANK, WIDTH])
+                gates[number] = [gate_pool.tile([P, TILES_PER_BANK, WIDTH], F32, name="gate") for t in range(BANKS)]
+                for t in range(BANKS):
+                    nc.vector.tensor_tensor(out=gates[number][t][:], in0=units[first_round + number]["sums"][t][:], in1=bias_cols, op=ALU.add)
 
-            group = closing(step - SUM_LAG)
-            if group is not None and group < HALVES:
-                half = group
-                cols = slice(half * ROWS, (half + 1) * ROWS)
-                cells[half] = [cell_pool.tile([P, ROWS], F32, name="cell") for b in range(BATCH_TILES)]
-                for b in range(BATCH_TILES):
-                    nc.vector.tensor_tensor(out=cells[half][b][:], in0=gates[group][b][:], in1=g_sb[:, b, cols], op=ALU.add)
+            number = round_at(step, SUM_LAG)
+            if number is not None and number < ROUNDS_PER_GATE:
+                cols = slice(number * WIDTH, (number + 1) * WIDTH)
+                cells[number] = [cell_pool.tile([P, TILES_PER_BANK, WIDTH], F32, name="cell") for t in range(BANKS)]
+                for t in range(BANKS):
+                    nc.vector.tensor_tensor(out=cells[number][t][:], in0=gates[number][t][:], in1=g_sb[:, rows_of(t), cols], op=ALU.add)
 
-            group = closing(step - SIGMOID_LAG)
-            if group is not None and group < HALVES:
-                half = group
-                cols = slice(half * ROWS, (half + 1) * ROWS)
-                for b in range(BATCH_TILES):
-                    nc.vector.tensor_tensor(out=gates[group][b][:], in0=gates[group][b][:], in1=c_sb[:, b, cols], op=ALU.mult)
-
-            group = closing(step - SIGMOID_LAG)
-            if group is not None and group >= HALVES:
-                half = group - HALVES
-                cols = slice(half * ROWS, (half + 1) * ROWS)
-                for b in range(BATCH_TILES):
-                    nc.vector.tensor_tensor(out=gates[group][b][:], in0=gates[group][b][:], in1=tanhs[half][b][:], op=ALU.mult)
-                    nc.sync.dma_start(out=out_0[b * P : (b + 1) * P, cols], in_=gates[group][b][:])
+            number = round_at(step, SIGMOID_LAG)
+            if number is not None and number < ROUNDS_PER_GATE:
+                cols = slice(number * WIDTH, (number + 1) * WIDTH)
+                for t in range(BANKS):
+                    nc.vector.tensor_tensor(out=gates[number][t][:], in0=gates[number][t][:], in1=c_sb[:, rows_of(t), cols], op=ALU.mult)
+            if number is not None and number >= ROUNDS_PER_GATE:
+                part = number - ROUNDS_PER_GATE
+                cols = slice(part * WIDTH, (part + 1) * WIDTH)
+                for t in range(BANKS):
+                    nc.vector.tensor_tensor(out=gates[number][t][:], in0=gates[number][t][:], in1=tanhs[part][t][:], op=ALU.mult)
+                    nc.sync.dma_start(out=out_h[:, rows_of(t), cols], in_=gates[number][t][:])

@@ -26,6 +26,7 @@ ROUNDS_PER_GATE = FEATURES // WIDTH
 ROUNDS = GATES * ROUNDS_PER_GATE
 BLOCKS = 4
 BANK = 512
+ROWS_PER_RUN = 2
 TILES_PER_BANK = BANK // WIDTH
 BANKS = BATCH_TILES // TILES_PER_BANK
 HEAD_UNITS = 3
@@ -75,35 +76,36 @@ def tile_lstmcell_pb_kernel(
         gate_weights = ((W_f, U_f), (W_o, U_o))
         units = []
         for name, matrix in (("x", incoming), ("h", h)):
-            blocks = [{"rows": matrix[i * P : (i + 1) * P, :], "slot": 0, "column": i * P} for i in range(BLOCKS)]
-            units.append({"name": name, "blocks": blocks, "slots": PASSES, "width": BATCH})
+            by_tile = matrix.rearrange("(p b) k -> p b k", b=BATCH_TILES)
+            loads = [by_tile[:, a * ROWS_PER_RUN : (a + 1) * ROWS_PER_RUN, :] for a in range(BLOCKS // ROWS_PER_RUN)]
+            blocks = [{"slot": 0, "column": i * P} for i in range(BLOCKS)]
+            units.append({"name": name, "loads": loads, "blocks": blocks, "slots": PASSES})
         for number in range(ROUNDS):
             gate, part = divmod(number, ROUNDS_PER_GATE)
-            blocks = []
-            for source in range(SOURCES):
-                for i in range(WIDTH // P):
-                    first = part * WIDTH + i * P
-                    blocks.append({"rows": gate_weights[gate][source][first : first + P, :], "slot": source * PASSES, "column": i * P})
-            units.append({"name": "r%d" % number, "blocks": blocks, "slots": SOURCES * PASSES, "width": WIDTH})
+            rows = slice(part * WIDTH, (part + 1) * WIDTH)
+            loads = [gate_weights[gate][source][rows, :].rearrange("(p t) k -> p t k", t=ROWS_PER_RUN) for source in range(SOURCES)]
+            blocks = [{"slot": source * PASSES, "column": t * P} for source in range(SOURCES) for t in range(ROWS_PER_RUN)]
+            units.append({"name": "r%d" % number, "loads": loads, "blocks": blocks, "slots": SOURCES * PASSES})
         first_round = len(units) - ROUNDS
 
         c_sb = raw_pool.tile([P, BATCH_TILES, FEATURES], BF16, name="c_sb")
         g_sb = raw_pool.tile([P, BATCH_TILES, FEATURES], BF16, name="g_sb")
         for index, unit in enumerate(units):
-            for i, block in enumerate(unit["blocks"]):
-                raw = raw_pool.tile([P, FEATURES], BF16, name="raw_%s_%d" % (unit["name"], i))
-                nc.sync.dma_start(out=raw[:], in_=block["rows"])
-                block["raw"] = raw
+            for a, rows in enumerate(unit["loads"]):
+                raw = raw_pool.tile([P, ROWS_PER_RUN, FEATURES], BF16, name="raw_%s_%d" % (unit["name"], a))
+                nc.sync.dma_start(out=raw[:], in_=rows)
+                for t in range(ROWS_PER_RUN):
+                    unit["blocks"][a * ROWS_PER_RUN + t]["raw"] = raw[:, t, :]
             if index == first_round + 1:
-                nc.sync.dma_start(out=c_sb[:], in_=c.rearrange("(b p) n -> p b n", p=P))
+                nc.sync.dma_start(out=c_sb[:], in_=c.rearrange("(p b) n -> p b n", b=BATCH_TILES))
             if index == first_round + 2:
-                nc.sync.dma_start(out=g_sb[:], in_=gated_cand.rearrange("(b p) n -> p b n", p=P))
+                nc.sync.dma_start(out=g_sb[:], in_=gated_cand.rearrange("(p b) n -> p b n", b=BATCH_TILES))
 
         def transpose_unit(unit, vector_copies):
             grouped = grouped_pool.tile([P, BLOCKS * FEATURES], BF16, name="grouped", align_bytes=64)
             grouped_words = grouped[:].bitcast(F32).rearrange("p (s r u) -> p s r u", s=unit["slots"], u=PAIRS)
             for i, block in enumerate(unit["blocks"]):
-                raw_words = block["raw"][:].bitcast(F32)
+                raw_words = block["raw"].bitcast(F32)
                 bank = transposed.tile([P, PASSES, PAIRS, P], F32, name="bank")
                 for g in range(PASSES):
                     for u in range(PAIRS):
@@ -152,8 +154,8 @@ def tile_lstmcell_pb_kernel(
             return slice(t * TILES_PER_BANK, (t + 1) * TILES_PER_BANK)
 
         bias_sb = const.tile([P, GATES * FEATURES], F32, name="bias_sb")
-        out_h = out_0.rearrange("(b p) n -> p b n", p=P)
-        out_c = out_1.rearrange("(b p) n -> p b n", p=P)
+        out_h = out_0.rearrange("(p b) n -> p b n", b=BATCH_TILES)
+        out_c = out_1.rearrange("(p b) n -> p b n", b=BATCH_TILES)
         gates = {}
         cells = {}
         tanhs = {}
@@ -188,10 +190,15 @@ def tile_lstmcell_pb_kernel(
                 quantise_unit(units[step], act_pool if step < first_round else weight_pool)
 
             if number is not None:
-                bias_cols = bias_sb[:, number * WIDTH : (number + 1) * WIDTH].unsqueeze(1).to_broadcast([P, TILES_PER_BANK, WIDTH])
+                bias_cols = bias_sb[:, number * WIDTH : (number + 1) * WIDTH].rearrange("p (r t) -> p r t", t=ROWS_PER_RUN)
                 gates[number] = [gate_pool.tile([P, TILES_PER_BANK, WIDTH], F32, name="gate") for t in range(BANKS)]
                 for t in range(BANKS):
-                    nc.vector.tensor_tensor(out=gates[number][t][:], in0=units[first_round + number]["sums"][t][:], in1=bias_cols, op=ALU.add)
+                    nc.vector.tensor_tensor(
+                        out=gates[number][t][:].rearrange("p j (r t) -> p j r t", t=ROWS_PER_RUN),
+                        in0=units[first_round + number]["sums"][t][:].rearrange("p j (t r) -> p j r t", t=ROWS_PER_RUN),
+                        in1=bias_cols.unsqueeze(1).to_broadcast([P, TILES_PER_BANK, WIDTH // ROWS_PER_RUN, ROWS_PER_RUN]),
+                        op=ALU.add,
+                    )
 
             number = round_at(step, SUM_LAG)
             if number is not None and number < ROUNDS_PER_GATE:

@@ -163,8 +163,8 @@ def tile_lstmcell_pb_kernel(
         for step in range(len(units) + SIGMOID_LAG):
             if step < len(units):
                 transpose_unit(units[step], SHARED_COPIES if step < HEAD_UNITS else 0)
-            if step == 0:
-                for q in range(GATES * FEATURES // BANK):
+            for q in range(GATES * FEATURES // BANK):
+                if step == 1 + q // (FEATURES // BANK):
                     bank = sums.tile([P, BANK], F32, name="sum")
                     nc.tensor.matmul(out=bank[:], lhsT=ones[:], rhs=bias_rows[:, q * BANK : (q + 1) * BANK], start=True, stop=True)
                     nc.scalar.copy(out=bias_sb[:, q * BANK : (q + 1) * BANK], in_=bank[:])
@@ -181,6 +181,13 @@ def tile_lstmcell_pb_kernel(
                 for t in range(BANKS):
                     nc.scalar.activation(out=tanhs[number][t][:], in_=cells[number][t][:], func=ACT.Tanh)
                     nc.sync.dma_start(out=out_c[:, rows_of(t), cols], in_=cells[number][t][:])
+
+            number = round_at(step, SUM_LAG)
+            if number is not None and number < ROUNDS_PER_GATE:
+                cols = slice(number * WIDTH, (number + 1) * WIDTH)
+                cells[number] = [cell_pool.tile([P, TILES_PER_BANK, WIDTH], F32, name="cell") for t in range(BANKS)]
+                for t in range(BANKS):
+                    nc.vector.tensor_tensor(out=cells[number][t][:], in0=gates[number][t][:], in1=g_sb[:, rows_of(t), cols], op=ALU.add)
 
             number = round_at(step, MULTIPLY_LAG)
             if number is not None:
@@ -199,13 +206,6 @@ def tile_lstmcell_pb_kernel(
                         in1=bias_cols.unsqueeze(1).to_broadcast([P, TILES_PER_BANK, WIDTH // ROWS_PER_RUN, ROWS_PER_RUN]),
                         op=ALU.add,
                     )
-
-            number = round_at(step, SUM_LAG)
-            if number is not None and number < ROUNDS_PER_GATE:
-                cols = slice(number * WIDTH, (number + 1) * WIDTH)
-                cells[number] = [cell_pool.tile([P, TILES_PER_BANK, WIDTH], F32, name="cell") for t in range(BANKS)]
-                for t in range(BANKS):
-                    nc.vector.tensor_tensor(out=cells[number][t][:], in0=gates[number][t][:], in1=g_sb[:, rows_of(t), cols], op=ALU.add)
 
             number = round_at(step, SIGMOID_LAG)
             if number is not None and number < ROUNDS_PER_GATE:

from contextlib import ExitStack

import concourse.mybir as mybir
from concourse.masks import make_identity

F32 = mybir.dt.float32
BF16 = mybir.dt.bfloat16
U32 = mybir.dt.uint32
U8 = mybir.dt.uint8
FP8X4 = mybir.dt.float8_e4m3fn_x4
ACT = mybir.ActivationFunctionType
ALU = mybir.AluOpType

P = 128
BATCH = 512
FEATURES = 1024
PACK = 4
K_PASS = P * PACK
PASSES = FEATURES // K_PASS
PAIRS = 2
SOURCES = 2
GATES = 2
BATCH_TILES = BATCH // P
WIDTH = 256
ROUNDS_PER_GATE = FEATURES // WIDTH
ROUNDS = GATES * ROUNDS_PER_GATE
BLOCKS = 4
BANK = 512
ROWS_PER_RUN = 2
TILES_PER_BANK = BANK // WIDTH
BANKS = BATCH_TILES // TILES_PER_BANK
HEAD_UNITS = 3
SHARED_COPIES = 2

MULTIPLY_LAG = 1
SIGMOID_LAG = 2
SUM_LAG = 3
TANH_LAG = 4

FLOPS = 2 * BATCH * (SOURCES * FEATURES) * (GATES * FEATURES)


def tile_lstmcell_pb_kernel(
    tc, incoming, h, c, gated_cand, W_f, b_W_f, W_o, b_W_o, U_f, b_U_f, U_o, b_U_o, out_0, out_1
):
    nc = tc.nc
    with ExitStack() as ctx:
        const = ctx.enter_context(tc.tile_pool(name="const", bufs=1))
        raw_pool = ctx.enter_context(tc.tile_pool(name="raw", bufs=1))
        grouped_pool = ctx.enter_context(tc.tile_pool(name="grouped", bufs=3))
        act_pool = ctx.enter_context(tc.tile_pool(name="act", bufs=SOURCES))
        weight_pool = ctx.enter_context(tc.tile_pool(name="weight", bufs=3))
        gate_pool = ctx.enter_context(tc.tile_pool(name="gate", bufs=10))
        cell_pool = ctx.enter_context(tc.tile_pool(name="cell", bufs=8))
        tanh_pool = ctx.enter_context(tc.tile_pool(name="tanh", bufs=8))
        transposed = ctx.enter_context(tc.psum_pool(name="transposed", bufs=4))
        sums = ctx.enter_context(tc.psum_pool(name="sums", bufs=4))
        ctx.enter_context(tc.manual_schedule())

        ident = const.tile([P, P], F32, name="ident")
        make_identity(nc, ident[:])
        ones = const.tile([P, P], BF16, name="ones")
        nc.vector.memset(ones[:], 1.0)
        warm = const.tile([P, 1], F32, name="warm")
        nc.vector.memset(warm[:], 0.0)
        nc.scalar.activation(out=warm[:], in_=warm[:], func=ACT.Sigmoid)
        bias_rows = const.tile([P, GATES * FEATURES], BF16, name="bias_rows")
        nc.vector.memset(bias_rows[:], 0.0)
        for gate, pair in enumerate(((b_W_f, b_U_f), (b_W_o, b_U_o))):
            for row, vector in enumerate(pair):
                nc.scalar.dma_start(
                    out=bias_rows[row : row + 1, gate * FEATURES : (gate + 1) * FEATURES],
                    in_=vector.rearrange("(o n) -> o n", o=1),
                )

        gate_weights = ((W_f, U_f), (W_o, U_o))
        units = []
        for name, matrix in (("x", incoming), ("h", h)):
            by_tile = matrix.rearrange("(p b) k -> p b k", b=BATCH_TILES)
            loads = [by_tile[:, a * ROWS_PER_RUN : (a + 1) * ROWS_PER_RUN, :] for a in range(BLOCKS // ROWS_PER_RUN)]
            blocks = [{"slot": 0, "column": i * P} for i in range(BLOCKS)]
            units.append({"name": name, "loads": loads, "blocks": blocks, "slots": PASSES})
        for number in range(ROUNDS):
            gate, part = divmod(number, ROUNDS_PER_GATE)
            rows = slice(part * WIDTH, (part + 1) * WIDTH)
            loads = [gate_weights[gate][source][rows, :].rearrange("(p t) k -> p t k", t=ROWS_PER_RUN) for source in range(SOURCES)]
            blocks = [{"slot": source * PASSES, "column": t * P} for source in range(SOURCES) for t in range(ROWS_PER_RUN)]
            units.append({"name": "r%d" % number, "loads": loads, "blocks": blocks, "slots": SOURCES * PASSES})
        first_round = len(units) - ROUNDS

        c_sb = raw_pool.tile([P, BATCH_TILES, FEATURES], BF16, name="c_sb")
        g_sb = raw_pool.tile([P, BATCH_TILES, FEATURES], BF16, name="g_sb")
        for index, unit in enumerate(units):
            for a, rows in enumerate(unit["loads"]):
                raw = raw_pool.tile([P, ROWS_PER_RUN, FEATURES], BF16, name="raw_%s_%d" % (unit["name"], a))
                nc.sync.dma_start(out=raw[:], in_=rows)
                for t in range(ROWS_PER_RUN):
                    unit["blocks"][a * ROWS_PER_RUN + t]["raw"] = raw[:, t, :]
            if index == first_round + 1:
                nc.sync.dma_start(out=c_sb[:], in_=c.rearrange("(p b) n -> p b n", b=BATCH_TILES))
            if index == first_round + 2:
                nc.sync.dma_start(out=g_sb[:], in_=gated_cand.rearrange("(p b) n -> p b n", b=BATCH_TILES))

        def transpose_unit(unit, vector_copies):
            grouped = grouped_pool.tile([P, BLOCKS * FEATURES], BF16, name="grouped", align_bytes=64)
            grouped_words = grouped[:].bitcast(F32).rearrange("p (s r u) -> p s r u", s=unit["slots"], u=PAIRS)
            for i, block in enumerate(unit["blocks"]):
                raw_words = block["raw"].bitcast(F32)
                bank = transposed.tile([P, PASSES, PAIRS, P], F32, name="bank")
                for g in range(PASSES):
                    for u in range(PAIRS):
                        first = (g * PAIRS + u) * P
                        nc.tensor.transpose(bank[:, g, u, :], raw_words[:, first : first + P], ident[:])
                copy_out = nc.vector.tensor_copy if i >= BLOCKS - vector_copies else nc.scalar.copy
                copy_out(
                    out=grouped_words[:, block["slot"] : block["slot"] + PASSES, block["column"] : block["column"] + P, :],
                    in_=bank[:].rearrange("p g u r -> p g r u"),
                )
            unit["grouped"] = grouped

        def quantise_unit(unit, pool):
            codes = pool.tile([P, BLOCKS * FEATURES // PACK], U32, name="codes", align_bytes=64)
            scales = pool.tile([P, BLOCKS * FEATURES // PACK], U8, name="scales", align_bytes=64)
            nc.vector.quantize_mx(out=codes[:].bitcast(FP8X4), scales=scales[:], in_=unit["grouped"][:])
            unit["codes"] = codes
            unit["scales"] = scales

        def multiply_round(unit):
            unit["sums"] = []
            for t in range(BANKS):
                bank = sums.tile([P, TILES_PER_BANK, WIDTH], F32, name="sum")
                for j in range(TILES_PER_BANK):
                    b = t * TILES_PER_BANK + j
                    for slot in range(SOURCES * PASSES):
                        source, g = divmod(slot, PASSES)
                        m_cols = slice(g * BATCH + b * P, g * BATCH + (b + 1) * P)
                        n_cols = slice(slot * WIDTH, (slot + 1) * WIDTH)
                        nc.tensor.matmul_mx(
                            out=bank[:, j, :],
                            lhsT=units[source]["codes"][:, m_cols].bitcast(FP8X4),
                            lhsT_scale=units[source]["scales"][:, m_cols],
                            rhs=unit["codes"][:, n_cols].bitcast(FP8X4),
                            rhs_scale=unit["scales"][:, n_cols],
                            start=(slot == 0),
                            stop=(slot == SOURCES * PASSES - 1),
                        )
                unit["sums"].append(bank)

        def round_at(step, lag):
            number = step - lag - first_round
            return number if 0 <= number < ROUNDS else None

        def rows_of(t):
            return slice(t * TILES_PER_BANK, (t + 1) * TILES_PER_BANK)

        bias_sb = const.tile([P, GATES * FEATURES], F32, name="bias_sb")
        out_h = out_0.rearrange("(p b) n -> p b n", b=BATCH_TILES)
        out_c = out_1.rearrange("(p b) n -> p b n", b=BATCH_TILES)
        gates = {}
        cells = {}
        tanhs = {}

        for step in range(len(units) + SIGMOID_LAG):
            if step < len(units):
                transpose_unit(units[step], SHARED_COPIES if step < HEAD_UNITS else 0)
            for q in range(GATES * FEATURES // BANK):
                if step == 1 + q // (FEATURES // BANK):
                    bank = sums.tile([P, BANK], F32, name="sum")
                    nc.tensor.matmul(out=bank[:], lhsT=ones[:], rhs=bias_rows[:, q * BANK : (q + 1) * BANK], start=True, stop=True)
                    nc.scalar.copy(out=bias_sb[:, q * BANK : (q + 1) * BANK], in_=bank[:])

            number = round_at(step, SIGMOID_LAG)
            if number is not None:
                for t in range(BANKS):
                    nc.scalar.activation(out=gates[number][t][:], in_=gates[number][t][:], func=ACT.Sigmoid)

            number = round_at(step, TANH_LAG)
            if number is not None and number < ROUNDS_PER_GATE:
                cols = slice(number * WIDTH, (number + 1) * WIDTH)
                tanhs[number] = [tanh_pool.tile([P, TILES_PER_BANK, WIDTH], F32, name="tanh_c") for t in range(BANKS)]
                for t in range(BANKS):
                    nc.scalar.activation(out=tanhs[number][t][:], in_=cells[number][t][:], func=ACT.Tanh)
                    nc.sync.dma_start(out=out_c[:, rows_of(t), cols], in_=cells[number][t][:])

            number = round_at(step, SUM_LAG)
            if number is not None and number < ROUNDS_PER_GATE:
                cols = slice(number * WIDTH, (number + 1) * WIDTH)
                cells[number] = [cell_pool.tile([P, TILES_PER_BANK, WIDTH], F32, name="cell") for t in range(BANKS)]
                for t in range(BANKS):
                    nc.vector.tensor_tensor(out=cells[number][t][:], in0=gates[number][t][:], in1=g_sb[:, rows_of(t), cols], op=ALU.add)

            number = round_at(step, MULTIPLY_LAG)
            if number is not None:
                multiply_round(units[first_round + number])

            if step < len(units):
                quantise_unit(units[step], act_pool if step < first_round else weight_pool)

            if number is not None:
                bias_cols = bias_sb[:, number * WIDTH : (number + 1) * WIDTH].rearrange("p (r t) -> p r t", t=ROWS_PER_RUN)
                gates[number] = [gate_pool.tile([P, TILES_PER_BANK, WIDTH], F32, name="gate") for t in range(BANKS)]
                for t in range(BANKS):
                    nc.vector.tensor_tensor(
                        out=gates[number][t][:].rearrange("p j (r t) -> p j r t", t=ROWS_PER_RUN),
                        in0=units[first_round + number]["sums"][t][:].rearrange("p j (t r) -> p j r t", t=ROWS_PER_RUN),
                        in1=bias_cols.unsqueeze(1).to_broadcast([P, TILES_PER_BANK, WIDTH // ROWS_PER_RUN, ROWS_PER_RUN]),
                        op=ALU.add,
                    )

            number = round_at(step, SIGMOID_LAG)
            if number is not None and number < ROUNDS_PER_GATE:
                cols = slice(number * WIDTH, (number + 1) * WIDTH)
                for t in range(BANKS):
                    nc.vector.tensor_tensor(out=gates[number][t][:], in0=gates[number][t][:], in1=c_sb[:, rows_of(t), cols], op=ALU.mult)
            if number is not None and number >= ROUNDS_PER_GATE:
                part = number - ROUNDS_PER_GATE
                cols = slice(part * WIDTH, (part + 1) * WIDTH)
                for t in range(BANKS):
                    nc.vector.tensor_tensor(out=gates[number][t][:], in0=gates[number][t][:], in1=tanhs[part][t][:], op=ALU.mult)
                    nc.sync.dma_start(out=out_h[:, rows_of(t), cols], in_=gates[number][t][:])
